import numpy as np
import ml_dtypes


def mxq(x, axis, fmt="e4m3"):
    dtype, down = {"e4m3": (ml_dtypes.float8_e4m3fn, 7), "e5m2": (ml_dtypes.float8_e5m2, 14)}[fmt]
    v = np.moveaxis(np.asarray(x, np.float32).astype(ml_dtypes.bfloat16).astype(np.float64), axis, -1)
    blocks = v.reshape(v.shape[:-1] + (-1, 32))
    amax = np.abs(blocks).max(-1, keepdims=True)
    byte = np.maximum(np.where(amax > 0, np.frexp(amax)[1] - 1 + 127, 0) - down, 1)
    scale = np.exp2(byte - 127.0)
    codes = (blocks / scale).astype(np.float32).astype(dtype).astype(np.float64)
    return np.moveaxis((codes * scale).reshape(v.shape), -1, axis)


WIDE = False


def mx_kscale(k):
    if not WIDE:
        return np.ones(k)
    levels = np.array([10, -10, 5, -5, 0])
    a = np.random.permutation(np.resize(levels, k // 512 * 4)).reshape(k // 512, 4)
    idx = np.arange(k)
    return np.exp2(a[idx // 512, idx % 128 // 32])


BF16 = ml_dtypes.bfloat16


def bf(x):
    return np.asarray(x, np.float32).astype(BF16)


def f64(x):
    return np.asarray(x).astype(np.float64)


N, I, O = 8192, 512, 128


def setup_inputs():
    s = mx_kscale(I)
    mask = np.tile(np.array([0.0, 0.0, 1.0, 1.0]), I // 4)
    gd = mask + 0.1 * (1.0 - mask)
    gs = (1.0 - mask) + 0.1 * mask
    x = np.random.standard_normal((N, I)) * s
    wd = np.random.standard_normal((O, I)) * gd / np.sqrt(I) / s
    ws = np.random.standard_normal((O, I)) * gs / np.sqrt(I) / s
    return {"x": bf(x), "W_dense": bf(wd), "W_sparse": bf(ws)}


def reference(x, W_dense, W_sparse):
    xq = mxq(f64(x), 1, "e4m3")
    out_dense = xq @ mxq(f64(W_dense), 1, "e4m3").T
    out_sparse = xq @ mxq(f64(W_sparse), 1, "e4m3").T
    return out_dense + out_sparse

@@ -1,0 +1,122 @@
+from contextlib import ExitStack
+
+import concourse.mybir as mybir
+from concourse.masks import make_identity
+
+F32 = mybir.dt.float32
+BF16 = mybir.dt.bfloat16
+U32 = mybir.dt.uint32
+U8 = mybir.dt.uint8
+FP8X4 = mybir.dt.float8_e4m3fn_x4
+
+P = 128
+N_ROWS, K, OUTS = 8192, 512, 128
+TILES = N_ROWS // P
+WORDS = K // 2
+FLOPS = 2 * 2 * N_ROWS * K * OUTS
+
+ROUNDS = [2, 2, 4, 8, 8, 8, 8, 8, 8, 4, 2, 2]
+LAG = 1
+
+
+def tile_myinterleavedmodule_t_kernel(tc, x, W_dense, W_sparse, out):
+    nc = tc.nc
+    assert sum(ROUNDS) == TILES
+    x_rows = x.rearrange("(p t) k -> p (t k)", t=TILES)
+    out_rows = out.rearrange("(p t) o -> p (t o)", t=TILES)
+    n = len(ROUNDS)
+    first = [sum(ROUNDS[:r]) for r in range(n)]
+
+    with ExitStack() as ctx:
+        const = ctx.enter_context(tc.tile_pool(name="const", bufs=1))
+        xin = ctx.enter_context(tc.tile_pool(name="xin", bufs=1))
+        gpool = ctx.enter_context(tc.tile_pool(name="gpool", bufs=3))
+        qpool = ctx.enter_context(tc.tile_pool(name="qpool", bufs=3))
+        opool = ctx.enter_context(tc.tile_pool(name="opool", bufs=3))
+        xt_pool = ctx.enter_context(tc.psum_pool(name="xtp", bufs=4))
+        acc_pool = ctx.enter_context(tc.psum_pool(name="accp", bufs=4))
+        ctx.enter_context(tc.manual_schedule())
+
+        ident = const.tile([P, P], F32, name="ident")
+        make_identity(nc, ident[:])
+
+        w_sb = const.tile([P, 2 * K], BF16, name="w_sb")
+        nc.sync.dma_start(out=w_sb[:, 0:K], in_=W_dense)
+        nc.sync.dma_start(out=w_sb[:, K : 2 * K], in_=W_sparse)
+        x_sb = []
+        for r in range(n):
+            xs = xin.tile([P, ROUNDS[r] * K], BF16, name="x%d" % r)
+            nc.sync.dma_start(out=xs[:], in_=x_rows[:, first[r] * K : (first[r] + ROUNDS[r]) * K])
+            x_sb.append(xs)
+
+        def transpose_pairs(src, tiles, grouped):
+            words = src[:].bitcast(F32)
+            g_words = grouped[:].bitcast(F32).rearrange("p (c u) -> p c u", u=2)
+            for b in range(tiles // 2):
+                xt = xt_pool.tile([P, 2, 2 * P], F32, name="xt")
+                for a in range(2):
+                    for u in range(2):
+                        col = (2 * b + a) * WORDS + u * P
+                        nc.tensor.transpose(xt[:, u, a * P : (a + 1) * P], words[:, col : col + P], ident[:])
+                nc.scalar.copy(
+                    out=g_words[:, 2 * b * P : (2 * b + 2) * P, :],
+                    in_=xt[:].rearrange("p u c -> p c u"),
+                )
+
+        def quantise(grouped, codes, scales, c0, c1):
+            nc.vector.quantize_mx(
+                out=codes[:, c0:c1].bitcast(FP8X4),
+                scales=scales[:, c0:c1],
+                in_=grouped[:, 4 * c0 : 4 * c1],
+            )
+
+        w_g = const.tile([P, 2 * P * 4], BF16, name="w_g", align_bytes=64)
+        w_codes = const.tile([P, 2 * P], U32, name="w_codes", align_bytes=64)
+        w_scales = const.tile([P, 2 * P], U8, name="w_scales", align_bytes=64)
+        transpose_pairs(w_sb, 2, w_g)
+        quantise(w_g, w_codes, w_scales, 0, 2 * P)
+
+        operands = {}
+        for step in range(n + LAG):
+            r, m = step, step - LAG
+            halves = []
+            if r < n:
+                cols = ROUNDS[r] * P
+                grouped = gpool.tile([P, cols * 4], BF16, name="grouped", align_bytes=64)
+                codes = qpool.tile([P, cols], U32, name="codes", align_bytes=64)
+                scales = qpool.tile([P, cols], U8, name="scales", align_bytes=64)
+                transpose_pairs(x_sb[r], ROUNDS[r], grouped)
+                operands[r] = (codes, scales)
+                halves = [(c, min(c + 4 * P, cols)) for c in range(0, cols, 4 * P)]
+            banks = []
+            if m >= 0:
+                m_codes, m_scales = operands[m]
+                o_sb = opool.tile([P, ROUNDS[m] * OUTS], F32, name="o_sb")
+                for t0 in range(0, ROUNDS[m], 4):
+                    nt = min(4, ROUNDS[m] - t0)
+                    acc = acc_pool.tile([P, 4 * OUTS], F32, name="acc")
+                    for j in range(nt):
+                        c = (t0 + j) * P
+                        for w in range(2):
+                            nc.tensor.matmul_mx(
+                                out=acc[:, j * OUTS : (j + 1) * OUTS],
+                                lhsT=m_codes[:, c : c + P].bitcast(FP8X4),
+                                lhsT_scale=m_scales[:, c : c + P],
+                                rhs=w_codes[:, w * P : (w + 1) * P].bitcast(FP8X4),
+                                rhs_scale=w_scales[:, w * P : (w + 1) * P],
+                                start=(w == 0),
+                                stop=(w == 1),
+                            )
+                    banks.append((acc, t0, nt))
+            for i in range(max(len(halves), len(banks))):
+                if i < len(halves):
+                    quantise(grouped, codes, scales, halves[i][0], halves[i][1])
+                if i < len(banks):
+                    acc, t0, nt = banks[i]
+                    nc.vector.tensor_copy(
+                        out=o_sb[:, t0 * OUTS : (t0 + nt) * OUTS], in_=acc[:, 0 : nt * OUTS]
+                    )
+            if m >= 0:
+                nc.sync.dma_start(
+                    out=out_rows[:, first[m] * OUTS : (first[m] + ROUNDS[m]) * OUTS], in_=o_sb[:]
+                )

@@ -32,7 +32,7 @@ def tile_myinterleavedmodule_t_kernel(tc, x, W_dense, W_sparse, out):
         xin = ctx.enter_context(tc.tile_pool(name="xin", bufs=1))
         gpool = ctx.enter_context(tc.tile_pool(name="gpool", bufs=3))
         qpool = ctx.enter_context(tc.tile_pool(name="qpool", bufs=3))
-        opool = ctx.enter_context(tc.tile_pool(name="opool", bufs=3))
+        opool = ctx.enter_context(tc.tile_pool(name="opool", bufs=1))
         xt_pool = ctx.enter_context(tc.psum_pool(name="xtp", bufs=4))
         acc_pool = ctx.enter_context(tc.psum_pool(name="accp", bufs=4))
         ctx.enter_context(tc.manual_schedule())
@@ -91,7 +91,7 @@ def tile_myinterleavedmodule_t_kernel(tc, x, W_dense, W_sparse, out):
             banks = []
             if m >= 0:
                 m_codes, m_scales = operands[m]
-                o_sb = opool.tile([P, ROUNDS[m] * OUTS], F32, name="o_sb")
+                o_sb = opool.tile([P, ROUNDS[m] * OUTS], F32, name="o%d" % m)
                 for t0 in range(0, ROUNDS[m], 4):
                     nt = min(4, ROUNDS[m] - t0)
                     acc = acc_pool.tile([P, 4 * OUTS], F32, name="acc")

@@ -16,7 +16,7 @@ WORDS = K // 2
 FLOPS = 2 * 2 * N_ROWS * K * OUTS
 
 ROUNDS = [2, 2, 4, 8, 8, 8, 8, 8, 8, 4, 2, 2]
-LAG = 1
+LAG = 2
 
 
 def tile_myinterleavedmodule_t_kernel(tc, x, W_dense, W_sparse, out):
@@ -31,7 +31,7 @@ def tile_myinterleavedmodule_t_kernel(tc, x, W_dense, W_sparse, out):
         const = ctx.enter_context(tc.tile_pool(name="const", bufs=1))
         xin = ctx.enter_context(tc.tile_pool(name="xin", bufs=1))
         gpool = ctx.enter_context(tc.tile_pool(name="gpool", bufs=3))
-        qpool = ctx.enter_context(tc.tile_pool(name="qpool", bufs=3))
+        qpool = ctx.enter_context(tc.tile_pool(name="qpool", bufs=4))
         opool = ctx.enter_context(tc.tile_pool(name="opool", bufs=1))
         xt_pool = ctx.enter_context(tc.psum_pool(name="xtp", bufs=4))
         acc_pool = ctx.enter_context(tc.psum_pool(name="accp", bufs=4))

@@ -15,8 +15,9 @@ TILES = N_ROWS // P
 WORDS = K // 2
 FLOPS = 2 * 2 * N_ROWS * K * OUTS
 
-ROUNDS = [2, 2, 4, 8, 8, 8, 8, 8, 8, 4, 2, 2]
+ROUNDS = [2, 2, 4, 4, 4, 8, 8, 8, 8, 8, 8]
 LAG = 2
+TAIL = 3
 
 
 def tile_myinterleavedmodule_t_kernel(tc, x, W_dense, W_sparse, out):
@@ -113,10 +114,16 @@ def tile_myinterleavedmodule_t_kernel(tc, x, W_dense, W_sparse, out):
                     quantise(grouped, codes, scales, halves[i][0], halves[i][1])
                 if i < len(banks):
                     acc, t0, nt = banks[i]
-                    nc.vector.tensor_copy(
-                        out=o_sb[:, t0 * OUTS : (t0 + nt) * OUTS], in_=acc[:, 0 : nt * OUTS]
-                    )
-            if m >= 0:
+                    o_part = o_sb[:, t0 * OUTS : (t0 + nt) * OUTS]
+                    if m >= n - TAIL and i % 2 == 1:
+                        nc.scalar.copy(out=o_part, in_=acc[:, 0 : nt * OUTS])
+                    else:
+                        nc.vector.tensor_copy(out=o_part, in_=acc[:, 0 : nt * OUTS])
+                    if m >= n - TAIL:
+                        nc.sync.dma_start(
+                            out=out_rows[:, (first[m] + t0) * OUTS : (first[m] + t0 + nt) * OUTS], in_=o_part
+                        )
+            if 0 <= m < n - TAIL:
                 nc.sync.dma_start(
                     out=out_rows[:, first[m] * OUTS : (first[m] + ROUNDS[m]) * OUTS], in_=o_sb[:]
                 )

@@ -15,9 +15,11 @@ TILES = N_ROWS // P
 WORDS = K // 2
 FLOPS = 2 * 2 * N_ROWS * K * OUTS
 
-ROUNDS = [2, 2, 4, 4, 4, 8, 8, 8, 8, 8, 8]
+ROUNDS = [2, 2, 4, 8, 8, 8, 8, 8, 8, 4, 2, 2]
 LAG = 2
-TAIL = 3
+IDLE_PLAIN_FIRST = 4
+IDLE_PLAIN_AFTER_STEP = {1: 2}
+IDLE_MX_AFTER_STEP = {2: 8, 3: 4}
 
 
 def tile_myinterleavedmodule_t_kernel(tc, x, W_dense, W_sparse, out):
@@ -40,6 +42,16 @@ def tile_myinterleavedmodule_t_kernel(tc, x, W_dense, W_sparse, out):
 
         ident = const.tile([P, P], F32, name="ident")
         make_identity(nc, ident[:])
+
+        zeros = const.tile([P, 4 * P], BF16, name="zeros")
+        nc.vector.memset(zeros[:], 0.0)
+
+        def idle_plain(count):
+            sink = acc_pool.tile([P, 4 * OUTS], F32, name="acc")
+            for i in range(count):
+                nc.tensor.matmul(out=sink[:], lhsT=zeros[:, 0:P], rhs=zeros[:], start=True, stop=True)
+
+        idle_plain(IDLE_PLAIN_FIRST)
 
         w_sb = const.tile([P, 2 * K], BF16, name="w_sb")
         nc.sync.dma_start(out=w_sb[:, 0:K], in_=W_dense)
@@ -77,6 +89,19 @@ def tile_myinterleavedmodule_t_kernel(tc, x, W_dense, W_sparse, out):
         transpose_pairs(w_sb, 2, w_g)
         quantise(w_g, w_codes, w_scales, 0, 2 * P)
 
+        def idle_mx(count):
+            sink = acc_pool.tile([P, 4 * OUTS], F32, name="acc")
+            for i in range(count):
+                nc.tensor.matmul_mx(
+                    out=sink[:, 0 : 2 * P],
+                    lhsT=w_codes[:, 0:P].bitcast(FP8X4),
+                    lhsT_scale=w_scales[:, 0:P],
+                    rhs=w_codes[:].bitcast(FP8X4),
+                    rhs_scale=w_scales[:],
+                    start=True,
+                    stop=True,
+                )
+
         operands = {}
         for step in range(n + LAG):
             r, m = step, step - LAG
@@ -109,21 +134,19 @@ def tile_myinterleavedmodule_t_kernel(tc, x, W_dense, W_sparse, out):
                                 stop=(w == 1),
                             )
                     banks.append((acc, t0, nt))
+            if step in IDLE_PLAIN_AFTER_STEP:
+                idle_plain(IDLE_PLAIN_AFTER_STEP[step])
+            if step in IDLE_MX_AFTER_STEP:
+                idle_mx(IDLE_MX_AFTER_STEP[step])
             for i in range(max(len(halves), len(banks))):
                 if i < len(halves):
                     quantise(grouped, codes, scales, halves[i][0], halves[i][1])
                 if i < len(banks):
                     acc, t0, nt = banks[i]
-                    o_part = o_sb[:, t0 * OUTS : (t0 + nt) * OUTS]
-                    if m >= n - TAIL and i % 2 == 1:
-                        nc.scalar.copy(out=o_part, in_=acc[:, 0 : nt * OUTS])
-                    else:
-                        nc.vector.tensor_copy(out=o_part, in_=acc[:, 0 : nt * OUTS])
-                    if m >= n - TAIL:
-                        nc.sync.dma_start(
-                            out=out_rows[:, (first[m] + t0) * OUTS : (first[m] + t0 + nt) * OUTS], in_=o_part
-                        )
-            if 0 <= m < n - TAIL:
+                    nc.vector.tensor_copy(
+                        out=o_sb[:, t0 * OUTS : (t0 + nt) * OUTS], in_=acc[:, 0 : nt * OUTS]
+                    )
+            if m >= 0:
                 nc.sync.dma_start(
                     out=out_rows[:, first[m] * OUTS : (first[m] + ROUNDS[m]) * OUTS], in_=o_sb[:]
                 )

@@ -15,11 +15,9 @@ TILES = N_ROWS // P
 WORDS = K // 2
 FLOPS = 2 * 2 * N_ROWS * K * OUTS
 
-ROUNDS = [2, 2, 4, 8, 8, 8, 8, 8, 8, 4, 2, 2]
+ROUNDS = [2, 2, 4, 8, 8, 8, 8, 8, 8, 8]
 LAG = 2
-IDLE_PLAIN_FIRST = 4
-IDLE_PLAIN_AFTER_STEP = {1: 2}
-IDLE_MX_AFTER_STEP = {2: 8, 3: 4}
+TAIL = 3
 
 
 def tile_myinterleavedmodule_t_kernel(tc, x, W_dense, W_sparse, out):
@@ -42,16 +40,6 @@ def tile_myinterleavedmodule_t_kernel(tc, x, W_dense, W_sparse, out):
 
         ident = const.tile([P, P], F32, name="ident")
         make_identity(nc, ident[:])
-
-        zeros = const.tile([P, 4 * P], BF16, name="zeros")
-        nc.vector.memset(zeros[:], 0.0)
-
-        def idle_plain(count):
-            sink = acc_pool.tile([P, 4 * OUTS], F32, name="acc")
-            for i in range(count):
-                nc.tensor.matmul(out=sink[:], lhsT=zeros[:, 0:P], rhs=zeros[:], start=True, stop=True)
-
-        idle_plain(IDLE_PLAIN_FIRST)
 
         w_sb = const.tile([P, 2 * K], BF16, name="w_sb")
         nc.sync.dma_start(out=w_sb[:, 0:K], in_=W_dense)
@@ -89,19 +77,6 @@ def tile_myinterleavedmodule_t_kernel(tc, x, W_dense, W_sparse, out):
         transpose_pairs(w_sb, 2, w_g)
         quantise(w_g, w_codes, w_scales, 0, 2 * P)
 
-        def idle_mx(count):
-            sink = acc_pool.tile([P, 4 * OUTS], F32, name="acc")
-            for i in range(count):
-                nc.tensor.matmul_mx(
-                    out=sink[:, 0 : 2 * P],
-                    lhsT=w_codes[:, 0:P].bitcast(FP8X4),
-                    lhsT_scale=w_scales[:, 0:P],
-                    rhs=w_codes[:].bitcast(FP8X4),
-                    rhs_scale=w_scales[:],
-                    start=True,
-                    stop=True,
-                )
-
         operands = {}
         for step in range(n + LAG):
             r, m = step, step - LAG
@@ -134,19 +109,21 @@ def tile_myinterleavedmodule_t_kernel(tc, x, W_dense, W_sparse, out):
                                 stop=(w == 1),
                             )
                     banks.append((acc, t0, nt))
-            if step in IDLE_PLAIN_AFTER_STEP:
-                idle_plain(IDLE_PLAIN_AFTER_STEP[step])
-            if step in IDLE_MX_AFTER_STEP:
-                idle_mx(IDLE_MX_AFTER_STEP[step])
             for i in range(max(len(halves), len(banks))):
                 if i < len(halves):
                     quantise(grouped, codes, scales, halves[i][0], halves[i][1])
                 if i < len(banks):
                     acc, t0, nt = banks[i]
-                    nc.vector.tensor_copy(
-                        out=o_sb[:, t0 * OUTS : (t0 + nt) * OUTS], in_=acc[:, 0 : nt * OUTS]
-                    )
-            if m >= 0:
+                    o_part = o_sb[:, t0 * OUTS : (t0 + nt) * OUTS]
+                    if m >= n - TAIL and i % 2 == 1:
+                        nc.scalar.copy(out=o_part, in_=acc[:, 0 : nt * OUTS])
+                    else:
+                        nc.vector.tensor_copy(out=o_part, in_=acc[:, 0 : nt * OUTS])
+                    if m >= n - TAIL:
+                        nc.sync.dma_start(
+                            out=out_rows[:, (first[m] + t0) * OUTS : (first[m] + t0 + nt) * OUTS], in_=o_part
+                        )
+            if 0 <= m < n - TAIL:
                 nc.sync.dma_start(
                     out=out_rows[:, first[m] * OUTS : (first[m] + ROUNDS[m]) * OUTS], in_=o_sb[:]
                 )

@@ -93,8 +93,11 @@ def tile_myinterleavedmodule_t_kernel(tc, x, W_dense, W_sparse, out):
             if m >= 0:
                 m_codes, m_scales = operands[m]
                 o_sb = opool.tile([P, ROUNDS[m] * OUTS], F32, name="o%d" % m)
-                for t0 in range(0, ROUNDS[m], 4):
-                    nt = min(4, ROUNDS[m] - t0)
+                starts = list(range(0, ROUNDS[m], 4))
+                if m == n - 1:
+                    starts.append(ROUNDS[m] - 2)
+                for t0, t1 in zip(starts, starts[1:] + [ROUNDS[m]]):
+                    nt = t1 - t0
                     acc = acc_pool.tile([P, 4 * OUTS], F32, name="acc")
                     for j in range(nt):
                         c = (t0 + j) * P

from contextlib import ExitStack

import concourse.mybir as mybir
from concourse.masks import make_identity

F32 = mybir.dt.float32
BF16 = mybir.dt.bfloat16
U32 = mybir.dt.uint32
U8 = mybir.dt.uint8
FP8X4 = mybir.dt.float8_e4m3fn_x4

P = 128
N_ROWS, K, OUTS = 8192, 512, 128
TILES = N_ROWS // P
WORDS = K // 2
FLOPS = 2 * 2 * N_ROWS * K * OUTS

ROUNDS = [2, 2, 4, 8, 8, 8, 8, 8, 8, 8]
LAG = 2
TAIL = 3


def tile_myinterleavedmodule_t_kernel(tc, x, W_dense, W_sparse, out):
    nc = tc.nc
    assert sum(ROUNDS) == TILES
    x_rows = x.rearrange("(p t) k -> p (t k)", t=TILES)
    out_rows = out.rearrange("(p t) o -> p (t o)", t=TILES)
    n = len(ROUNDS)
    first = [sum(ROUNDS[:r]) for r in range(n)]

    with ExitStack() as ctx:
        const = ctx.enter_context(tc.tile_pool(name="const", bufs=1))
        xin = ctx.enter_context(tc.tile_pool(name="xin", bufs=1))
        gpool = ctx.enter_context(tc.tile_pool(name="gpool", bufs=3))
        qpool = ctx.enter_context(tc.tile_pool(name="qpool", bufs=4))
        opool = ctx.enter_context(tc.tile_pool(name="opool", bufs=1))
        xt_pool = ctx.enter_context(tc.psum_pool(name="xtp", bufs=4))
        acc_pool = ctx.enter_context(tc.psum_pool(name="accp", bufs=4))
        ctx.enter_context(tc.manual_schedule())

        ident = const.tile([P, P], F32, name="ident")
        make_identity(nc, ident[:])

        w_sb = const.tile([P, 2 * K], BF16, name="w_sb")
        nc.sync.dma_start(out=w_sb[:, 0:K], in_=W_dense)
        nc.sync.dma_start(out=w_sb[:, K : 2 * K], in_=W_sparse)
        x_sb = []
        for r in range(n):
            xs = xin.tile([P, ROUNDS[r] * K], BF16, name="x%d" % r)
            nc.sync.dma_start(out=xs[:], in_=x_rows[:, first[r] * K : (first[r] + ROUNDS[r]) * K])
            x_sb.append(xs)

        def transpose_pairs(src, tiles, grouped):
            words = src[:].bitcast(F32)
            g_words = grouped[:].bitcast(F32).rearrange("p (c u) -> p c u", u=2)
            for b in range(tiles // 2):
                xt = xt_pool.tile([P, 2, 2 * P], F32, name="xt")
                for a in range(2):
                    for u in range(2):
                        col = (2 * b + a) * WORDS + u * P
                        nc.tensor.transpose(xt[:, u, a * P : (a + 1) * P], words[:, col : col + P], ident[:])
                nc.scalar.copy(
                    out=g_words[:, 2 * b * P : (2 * b + 2) * P, :],
                    in_=xt[:].rearrange("p u c -> p c u"),
                )

        def quantise(grouped, codes, scales, c0, c1):
            nc.vector.quantize_mx(
                out=codes[:, c0:c1].bitcast(FP8X4),
                scales=scales[:, c0:c1],
                in_=grouped[:, 4 * c0 : 4 * c1],
            )

        w_g = const.tile([P, 2 * P * 4], BF16, name="w_g", align_bytes=64)
        w_codes = const.tile([P, 2 * P], U32, name="w_codes", align_bytes=64)
        w_scales = const.tile([P, 2 * P], U8, name="w_scales", align_bytes=64)
        transpose_pairs(w_sb, 2, w_g)
        quantise(w_g, w_codes, w_scales, 0, 2 * P)

        operands = {}
        for step in range(n + LAG):
            r, m = step, step - LAG
            halves = []
            if r < n:
                cols = ROUNDS[r] * P
                grouped = gpool.tile([P, cols * 4], BF16, name="grouped", align_bytes=64)
                codes = qpool.tile([P, cols], U32, name="codes", align_bytes=64)
                scales = qpool.tile([P, cols], U8, name="scales", align_bytes=64)
                transpose_pairs(x_sb[r], ROUNDS[r], grouped)
                operands[r] = (codes, scales)
                halves = [(c, min(c + 4 * P, cols)) for c in range(0, cols, 4 * P)]
            banks = []
            if m >= 0:
                m_codes, m_scales = operands[m]
                o_sb = opool.tile([P, ROUNDS[m] * OUTS], F32, name="o%d" % m)
                starts = list(range(0, ROUNDS[m], 4))
                if m == n - 1:
                    starts.append(ROUNDS[m] - 2)
                for t0, t1 in zip(starts, starts[1:] + [ROUNDS[m]]):
                    nt = t1 - t0
                    acc = acc_pool.tile([P, 4 * OUTS], F32, name="acc")
                    for j in range(nt):
                        c = (t0 + j) * P
                        for w in range(2):
                            nc.tensor.matmul_mx(
                                out=acc[:, j * OUTS : (j + 1) * OUTS],
                                lhsT=m_codes[:, c : c + P].bitcast(FP8X4),
                                lhsT_scale=m_scales[:, c : c + P],
                                rhs=w_codes[:, w * P : (w + 1) * P].bitcast(FP8X4),
                                rhs_scale=w_scales[:, w * P : (w + 1) * P],
                                start=(w == 0),
                                stop=(w == 1),
                            )
                    banks.append((acc, t0, nt))
            for i in range(max(len(halves), len(banks))):
                if i < len(halves):
                    quantise(grouped, codes, scales, halves[i][0], halves[i][1])
                if i < len(banks):
                    acc, t0, nt = banks[i]
                    o_part = o_sb[:, t0 * OUTS : (t0 + nt) * OUTS]
                    if m >= n - TAIL and i % 2 == 1:
                        nc.scalar.copy(out=o_part, in_=acc[:, 0 : nt * OUTS])
                    else:
                        nc.vector.tensor_copy(out=o_part, in_=acc[:, 0 : nt * OUTS])
                    if m >= n - TAIL:
                        nc.sync.dma_start(
                            out=out_rows[:, (first[m] + t0) * OUTS : (first[m] + t0 + nt) * OUTS], in_=o_part
                        )
            if 0 <= m < n - TAIL:
                nc.sync.dma_start(
                    out=out_rows[:, first[m] * OUTS : (first[m] + ROUNDS[m]) * OUTS], in_=o_sb[:]
                )
